import numpy as np
import ml_dtypes


def mxq(x, axis, fmt="e4m3"):
    dtype, down = {"e4m3": (ml_dtypes.float8_e4m3fn, 7), "e5m2": (ml_dtypes.float8_e5m2, 14)}[fmt]
    v = np.moveaxis(np.asarray(x, np.float32).astype(ml_dtypes.bfloat16).astype(np.float64), axis, -1)
    blocks = v.reshape(v.shape[:-1] + (-1, 32))
    amax = np.abs(blocks).max(-1, keepdims=True)
    byte = np.maximum(np.where(amax > 0, np.frexp(amax)[1] - 1 + 127, 0) - down, 1)
    scale = np.exp2(byte - 127.0)
    codes = (blocks / scale).astype(np.float32).astype(dtype).astype(np.float64)
    return np.moveaxis((codes * scale).reshape(v.shape), -1, axis)


WIDE = False


def mx_kscale(k):
    if not WIDE:
        return np.ones(k)
    levels = np.array([10, -10, 5, -5, 0])
    a = np.random.permutation(np.resize(levels, k // 512 * 4)).reshape(k // 512, 4)
    idx = np.arange(k)
    return np.exp2(a[idx // 512, idx % 128 // 32])


BF16 = ml_dtypes.bfloat16


def bf(x):
    return np.asarray(x, np.float32).astype(BF16)


def f64(x):
    return np.asarray(x).astype(np.float64)


E2M1 = np.array([0.0, 0.5, 1.0, 1.5, 2.0, 3.0, 4.0, 6.0, -0.0, -0.5, -1.0, -1.5, -2.0, -3.0, -4.0, -6.0])


def pack_weight(w, fmt):
    k, n = w.shape
    w = f64(bf(w)).reshape(k // 32, 32, n)
    amax = np.abs(w).max(1)
    if fmt == "e4m3":
        byte = np.frexp(amax)[1] - 1 + 127 - 7
    else:
        mant, ex = np.frexp(amax / 6.0)
        byte = np.where(mant > 0.5, ex, ex - 1) + 127
    byte = np.clip(np.where(amax > 0, byte, 1), 1, 254)
    scaled = (w * np.exp2(127.0 - byte)[:, None, :]).reshape(k, n).astype(np.float32)
    by_word = np.ascontiguousarray(scaled.reshape(k // 512, 128, 4, n).transpose(0, 1, 3, 2))
    if fmt == "e4m3":
        words = by_word.astype(ml_dtypes.float8_e4m3fn).view(np.uint8)
    else:
        c = by_word.astype(ml_dtypes.float4_e2m1fn).view(np.uint8) & 0xF
        words = c[..., 0::2] | (c[..., 1::2] << 4)
    return np.ascontiguousarray(words), np.ascontiguousarray(byte.astype(np.uint8).reshape(k // 512, 16, n))


def unpack_weight(words, scales, fmt):
    g, p, n, _ = words.shape
    if fmt == "e4m3":
        vals = np.ascontiguousarray(words).view(ml_dtypes.float8_e4m3fn).astype(np.float64)
    else:
        nib = np.empty((g, p, n, 4), np.uint8)
        nib[..., 0::2] = words & 0xF
        nib[..., 1::2] = words >> 4
        vals = E2M1[nib]
    vals = vals * np.repeat(np.exp2(scales.astype(np.float64) - 127.0), 8, axis=1)[..., None]
    return vals.transpose(0, 1, 3, 2).reshape(g * 512, n)


B, IN, HID, PROJ, H, KC = 128, 2048, 2048, 2048, 4, 4
BH = HID // H
BI = PROJ // H
FMT = "e4m3"


def sigmoid(v):
    return 1.0 / (1.0 + np.exp(-v))


def silu(v):
    return v / (1.0 + np.exp(-v))


def blockdiag(vq, w, b):
    y = vq.reshape(B, H, BI).transpose(1, 0, 2) @ mxq(f64(w), 1, "e4m3")
    return y.transpose(1, 0, 2).reshape(B, HID) + f64(b)


def setup_inputs():
    s, t = mx_kscale(PROJ), mx_kscale(PROJ)
    sh, th = s.reshape(H, BI, 1), t.reshape(H, BI, 1)
    r = np.random.standard_normal
    d = {"x_conv": bf(silu(r((B, PROJ))) * s), "x_left": bf(r((B, PROJ)) * t),
         "c_prev": bf(r((B, HID))), "n_prev": bf(r((B, HID))), "m_prev": bf(0.5 * r((B, HID))),
         "wq_w": bf(r((H, BI, BH)) * 1.5 / np.sqrt(BI) / sh), "wq_b": bf(0.2 * r(HID)),
         "wk_w": bf(r((H, BI, BH)) * 0.5 * np.sqrt(BH) / np.sqrt(BI) / sh), "wk_b": bf(0.1 * np.sqrt(BH) * r(HID)),
         "wv_w": bf(r((H, BI, BH)) / np.sqrt(BI) / th), "wv_b": bf(0.2 * r(HID))}
    d["wi_w_words"], d["wi_w_scales"] = pack_weight(r((PROJ, HID)) * 1.5 / np.sqrt(PROJ) / s[:, None], FMT)
    d["wi_b"] = bf(0.2 * r(HID))
    d["wf_w_words"], d["wf_w_scales"] = pack_weight(r((PROJ, HID)) * 1.5 / np.sqrt(PROJ) / s[:, None], FMT)
    d["wf_b"] = bf(0.2 * r(HID))
    d["wo_w_words"], d["wo_w_scales"] = pack_weight(r((PROJ, HID)) / np.sqrt(PROJ) / t[:, None], FMT)
    d["wo_b"] = bf(0.2 * r(HID))
    return d


def reference(x_conv, x_left, c_prev, n_prev, m_prev, wq_w, wq_b, wk_w, wk_b, wv_w, wv_b, wi_w_words, wi_w_scales, wi_b, wf_w_words, wf_w_scales, wf_b, wo_w_words, wo_w_scales, wo_b):
    xc = mxq(f64(x_conv), 1, "e4m3")
    xl = mxq(f64(x_left), 1, "e4m3")
    q = blockdiag(xc, wq_w, wq_b)
    k = blockdiag(xc, wk_w, wk_b) / np.sqrt(BH)
    v = blockdiag(xl, wv_w, wv_b)
    i_tilde = (xc @ unpack_weight(wi_w_words, wi_w_scales, FMT)) + f64(wi_b)
    f_tilde = (xc @ unpack_weight(wf_w_words, wf_w_scales, FMT)) + f64(wf_b)
    o = sigmoid((xl @ unpack_weight(wo_w_words, wo_w_scales, FMT)) + f64(wo_b))
    m_t = np.maximum(f_tilde + f64(m_prev), i_tilde)
    i = np.exp(i_tilde - m_t)
    f = np.exp(f_tilde + f64(m_prev) - m_t)
    c_t = f * f64(c_prev) + i * (v * k)
    n_t = f * f64(n_prev) + i * k
    denom = np.sqrt(np.sum((n_t * q) ** 2, axis=-1, keepdims=True)) + 1e-6
    h_t = o * (c_t * q) / denom
    return h_t, c_t, n_t, m_t

@@ -1,0 +1,307 @@
+from contextlib import ExitStack
+import math
+
+import concourse.mybir as mybir
+from concourse.masks import make_identity
+
+F32 = mybir.dt.float32
+BF16 = mybir.dt.bfloat16
+I32 = mybir.dt.int32
+U32 = mybir.dt.uint32
+U8 = mybir.dt.uint8
+FP8X4 = mybir.dt.float8_e4m3fn_x4
+ALU = mybir.AluOpType
+ACT = mybir.ActivationFunctionType
+
+P = 128
+PACK = 4
+K_PASS = P * PACK
+HEADS = 4
+HEAD = 512
+D = HEADS * HEAD
+PASSES = D // K_PASS
+QUADS = 4
+LIVE = 4
+
+BQ, BK, BV, BI, BF, BO = range(6)
+
+FLOPS = 2 * P * (3 * D * D + 3 * HEADS * HEAD * HEAD)
+
+
+def tile_mlstmblock_pb_kernel(
+    tc,
+    x_conv, x_left, c_prev, n_prev, m_prev,
+    wq_w, wq_b, wk_w, wk_b, wv_w, wv_b,
+    wi_w_words, wi_w_scales, wi_b,
+    wf_w_words, wf_w_scales, wf_b,
+    wo_w_words, wo_w_scales, wo_b,
+    out_0, out_1, out_2, out_3,
+):
+    nc = tc.nc
+    h_out, c_out, n_out, m_out = out_0, out_1, out_2, out_3
+
+    with ExitStack() as ctx:
+        const = ctx.enter_context(tc.tile_pool(name="const", bufs=1))
+        raw_pool = ctx.enter_context(tc.tile_pool(name="raw", bufs=6))
+        grouped_pool = ctx.enter_context(tc.tile_pool(name="grouped", bufs=3))
+        head_w_pool = ctx.enter_context(tc.tile_pool(name="head_w", bufs=4))
+        packed_pool = ctx.enter_context(tc.tile_pool(name="packed", bufs=8))
+        work = ctx.enter_context(tc.tile_pool(name="work", bufs=2))
+        stored = ctx.enter_context(tc.tile_pool(name="stored", bufs=3))
+        acc_pool = ctx.enter_context(tc.psum_pool(name="acc", bufs=6))
+        aux_pool = ctx.enter_context(tc.psum_pool(name="aux", bufs=2))
+
+        def load_rows(src):
+            rows = raw_pool.tile([P, D], BF16, tag="raw")
+            nc.sync.dma_start(out=rows[:], in_=src)
+            return rows
+
+        def load_head_weight(w, h):
+            raw = raw_pool.tile([P, PACK, HEAD], BF16, tag="raw")
+            nc.sync.dma_start(out=raw[:], in_=w[h].rearrange("(p t) o -> p t o", t=PACK))
+            return raw
+
+        def load_packed_columns(words, h):
+            packed = packed_pool.tile([P, PASSES, HEAD], I32, tag="packed", align_bytes=64)
+            by_partition = words.rearrange("g p n t -> p g (n t)")
+            nc.sync.dma_start(
+                out=packed[:],
+                in_=by_partition[:, :, PACK * HEAD * h : PACK * HEAD * (h + 1)].bitcast(I32),
+            )
+            return packed
+
+        def load_scale_planes(scales, planes):
+            for quad in range(QUADS):
+                nc.sync.dma_start(
+                    out=planes[32 * quad : 32 * quad + PASSES * LIVE, :].bitcast(I32),
+                    in_=scales[:, LIVE * quad : LIVE * (quad + 1), :].bitcast(I32),
+                )
+
+        ident_f32 = const.tile([P, P], F32)
+        make_identity(nc, ident_f32[:])
+        ident_bf16 = const.tile([P, P], BF16)
+        make_identity(nc, ident_bf16[:])
+        half = const.tile([P, 1], F32)
+        nc.vector.memset(half[:], 0.5)
+
+        bias_rows = const.tile([P, HEAD], BF16)
+        nc.vector.memset(bias_rows[:], 0.0)
+        for j, bias in enumerate((wq_b, wk_b, wv_b, wi_b, wf_b, wo_b)):
+            nc.sync.dma_start(
+                out=bias_rows[HEADS * j : HEADS * (j + 1), :],
+                in_=bias.rearrange("(h c) -> h c", c=HEAD),
+            )
+
+        planes_i = const.tile([P, D], U8, align_bytes=64)
+        planes_f = const.tile([P, D], U8, align_bytes=64)
+        planes_o = const.tile([P, D], U8, align_bytes=64)
+        for planes in (planes_i, planes_f, planes_o):
+            nc.vector.memset(planes[:].bitcast(I32), 0)
+
+        xc_rows = load_rows(x_conv)
+        xl_rows = load_rows(x_left)
+        m_rows = load_rows(m_prev)
+        head_raw = {}
+        gate_packed = {}
+
+        def load_head(h):
+            head_raw[h] = (
+                load_head_weight(wk_w, h),
+                load_head_weight(wv_w, h),
+                load_head_weight(wq_w, h),
+            )
+            if h == 0:
+                load_scale_planes(wi_w_scales, planes_i)
+                load_scale_planes(wf_w_scales, planes_f)
+                load_scale_planes(wo_w_scales, planes_o)
+            gate_packed[h] = (
+                load_packed_columns(wi_w_words, h),
+                load_packed_columns(wf_w_words, h),
+            )
+
+        load_head(0)
+        c_rows = const.tile([P, D], BF16)
+        nc.sync.dma_start(out=c_rows[:], in_=c_prev)
+        n_rows = const.tile([P, D], BF16)
+        nc.sync.dma_start(out=n_rows[:], in_=n_prev)
+
+        def quantise_rows(rows, codes, plane):
+            words = rows[:].bitcast(F32)
+            grouped = grouped_pool.tile([P, D], BF16, tag="grouped", align_bytes=64)
+            grouped_words = grouped[:].bitcast(F32).rearrange(
+                "p (g b u) -> p g b u", g=PASSES, u=2
+            )
+            for pair in range(PASSES // 2):
+                turned = aux_pool.tile([P, 2, 2, P], F32, tag="aux")
+                for i in range(2):
+                    g = 2 * pair + i
+                    for u in range(2):
+                        nc.tensor.transpose(
+                            out=turned[:, i, u, :],
+                            in_=words[:, 256 * g + u : 256 * (g + 1) : 2],
+                            identity=ident_f32[:],
+                        )
+                copy = nc.scalar.copy if pair == 0 else nc.vector.tensor_copy
+                copy(
+                    out=grouped_words[:, 2 * pair : 2 * pair + 2, :, :],
+                    in_=turned[:].rearrange("p g u b -> p g b u"),
+                )
+            nc.vector.quantize_mx(out=codes[:].bitcast(FP8X4), scales=plane[:], in_=grouped[:])
+
+        xc_codes = const.tile([P, PASSES * P], U32, align_bytes=64)
+        xc_plane = const.tile([P, PASSES * P], U8, align_bytes=64)
+        quantise_rows(xc_rows, xc_codes, xc_plane)
+        xl_codes = const.tile([P, PASSES * P], U32, align_bytes=64)
+        xl_plane = const.tile([P, PASSES * P], U8, align_bytes=64)
+        quantise_rows(xl_rows, xl_codes, xl_plane)
+
+        bias_all = const.tile([P, HEADS, 6, HEAD], BF16)
+        for h in range(HEADS):
+            for pair in range(3):
+                spread = aux_pool.tile([P, 2, HEAD], BF16, tag="aux")
+                for i in range(2):
+                    row = HEADS * (2 * pair + i) + h
+                    nc.tensor.matmul(
+                        out=spread[:, i, :],
+                        lhsT=ident_bf16[:, row : row + 1].to_broadcast([P, P]),
+                        rhs=bias_rows[:],
+                        start=True,
+                        stop=True,
+                    )
+                copy = nc.scalar.copy if (3 * h + pair) % 2 == 0 else nc.vector.tensor_copy
+                copy(out=bias_all[:, h, 2 * pair : 2 * pair + 2, :], in_=spread[:])
+
+        fbias_m = const.tile([P, D], F32)
+        for h in range(HEADS):
+            cols = slice(HEAD * h, HEAD * (h + 1))
+            nc.vector.tensor_tensor(
+                out=fbias_m[:, cols], in0=m_rows[:, cols], in1=bias_all[:, h, BF, :], op=ALU.add
+            )
+
+        def project_head(raw, x_codes, x_plane, h):
+            grouped = grouped_pool.tile([P, PACK * HEAD], BF16, tag="grouped", align_bytes=64)
+            nc.scalar.copy(
+                out=grouped[:].rearrange("p (c i t) -> p c t i", i=4, t=PACK),
+                in_=raw[:].rearrange("p t (c i) -> p c t i", i=4),
+            )
+            codes = head_w_pool.tile([P, HEAD], U32, tag="codes", align_bytes=64)
+            plane = head_w_pool.tile([P, HEAD], U8, tag="plane", align_bytes=64)
+            nc.vector.quantize_mx(out=codes[:].bitcast(FP8X4), scales=plane[:], in_=grouped[:])
+            acc = acc_pool.tile([P, HEAD], F32, tag="acc")
+            rows = slice(P * h, P * (h + 1))
+            nc.tensor.matmul_mx(
+                out=acc[:],
+                lhsT=x_codes[:, rows].bitcast(FP8X4),
+                lhsT_scale=x_plane[:, rows],
+                rhs=codes[:].bitcast(FP8X4),
+                rhs_scale=plane[:],
+                start=True,
+                stop=True,
+            )
+            return acc
+
+        def project_full(packed, planes, x_codes, x_plane, h):
+            acc = acc_pool.tile([P, HEAD], F32, tag="acc")
+            for g in range(PASSES):
+                rows = slice(P * g, P * (g + 1))
+                nc.tensor.matmul_mx(
+                    out=acc[:],
+                    lhsT=x_codes[:, rows].bitcast(FP8X4),
+                    lhsT_scale=x_plane[:, rows],
+                    rhs=packed[:, g, :].bitcast(FP8X4),
+                    rhs_scale=planes[LIVE * g : P, HEAD * h : HEAD * (h + 1)],
+                    start=(g == 0),
+                    stop=(g == PASSES - 1),
+                )
+            return acc
+
+        def add_bias(acc, h, which, tag):
+            biased = work.tile([P, HEAD], F32, tag=tag)
+            nc.vector.tensor_tensor(
+                out=biased[:], in0=acc[:], in1=bias_all[:, h, which, :], op=ALU.add
+            )
+            return biased
+
+        cq_all = const.tile([P, D], F32)
+        square_sums = const.tile([P, HEADS], F32)
+
+        def update_head(h):
+            cols = slice(HEAD * h, HEAD * (h + 1))
+            k_raw, v_raw, q_raw = head_raw[h]
+            i_packed, f_packed = gate_packed[h]
+            k_acc = project_head(k_raw, xc_codes, xc_plane, h)
+            v_acc = project_head(v_raw, xl_codes, xl_plane, h)
+            q_acc = project_head(q_raw, xc_codes, xc_plane, h)
+            i_acc = project_full(i_packed, planes_i, xc_codes, xc_plane, h)
+            f_acc = project_full(f_packed, planes_f, xc_codes, xc_plane, h)
+
+            k = add_bias(k_acc, h, BK, "k")
+            v = add_bias(v_acc, h, BV, "v")
+            q = add_bias(q_acc, h, BQ, "q")
+            i_gate = add_bias(i_acc, h, BI, "i_gate")
+            f_gate = work.tile([P, HEAD], F32, tag="f_gate")
+            nc.vector.tensor_tensor(
+                out=f_gate[:], in0=f_acc[:], in1=fbias_m[:, cols], op=ALU.add
+            )
+
+            m_t = stored.tile([P, HEAD], F32, tag="m_t")
+            nc.vector.tensor_tensor(out=m_t[:], in0=f_gate[:], in1=i_gate[:], op=ALU.max)
+            nc.sync.dma_start(out=m_out[:, cols], in_=m_t[:])
+
+            nc.vector.tensor_tensor(out=i_gate[:], in0=i_gate[:], in1=m_t[:], op=ALU.subtract)
+            nc.vector.tensor_tensor(out=f_gate[:], in0=f_gate[:], in1=m_t[:], op=ALU.subtract)
+            nc.scalar.activation(out=i_gate[:], in_=i_gate[:], func=ACT.Exp)
+            nc.scalar.activation(out=f_gate[:], in_=f_gate[:], func=ACT.Exp)
+
+            nc.vector.scalar_tensor_tensor(
+                out=k[:], in0=k[:], scalar=1.0 / math.sqrt(HEAD), in1=i_gate[:],
+                op0=ALU.mult, op1=ALU.mult,
+            )
+            nc.vector.tensor_tensor(out=v[:], in0=v[:], in1=k[:], op=ALU.mult)
+
+            c_t = stored.tile([P, HEAD], F32, tag="c_t")
+            nc.vector.tensor_tensor(out=c_t[:], in0=f_gate[:], in1=c_rows[:, cols], op=ALU.mult)
+            n_t = stored.tile([P, HEAD], F32, tag="n_t")
+            nc.vector.tensor_tensor(out=n_t[:], in0=f_gate[:], in1=n_rows[:, cols], op=ALU.mult)
+            nc.vector.tensor_tensor(out=c_t[:], in0=c_t[:], in1=v[:], op=ALU.add)
+            nc.vector.tensor_tensor(out=n_t[:], in0=n_t[:], in1=k[:], op=ALU.add)
+            nc.sync.dma_start(out=c_out[:, cols], in_=c_t[:])
+            nc.sync.dma_start(out=n_out[:, cols], in_=n_t[:])
+
+            nq = work.tile([P, HEAD], F32, tag="nq")
+            nc.vector.tensor_tensor(out=nq[:], in0=n_t[:], in1=q[:], op=ALU.mult)
+            nc.scalar.activation(
+                out=nq[:], in_=nq[:], func=ACT.Square, accum_out=square_sums[:, h : h + 1]
+            )
+            nc.vector.tensor_tensor(out=cq_all[:, cols], in0=c_t[:], in1=q[:], op=ALU.mult)
+
+        load_head(1)
+        update_head(0)
+        load_head(2)
+        update_head(1)
+        load_head(3)
+        o_packed = [load_packed_columns(wo_w_words, h) for h in range(HEADS)]
+        update_head(2)
+        update_head(3)
+
+        total = const.tile([P, 1], F32)
+        nc.vector.tensor_reduce(
+            out=total[:], in_=square_sums[:], axis=mybir.AxisListType.X, op=ALU.add
+        )
+        denom = const.tile([P, 1], F32)
+        nc.gpsimd.tensor_tensor(out=denom[:], in0=total[:], in1=half[:], op=ALU.pow)
+        nc.vector.tensor_scalar_add(out=denom[:], in0=denom[:], scalar1=1e-6)
+        inv_denom = const.tile([P, 1], F32)
+        nc.vector.reciprocal(out=inv_denom[:], in_=denom[:])
+
+        for h in range(HEADS):
+            cols = slice(HEAD * h, HEAD * (h + 1))
+            o_acc = project_full(o_packed[h], planes_o, xl_codes, xl_plane, h)
+            o_gate = add_bias(o_acc, h, BO, "o_gate")
+            nc.scalar.activation(out=o_gate[:], in_=o_gate[:], func=ACT.Sigmoid)
+            h_t = stored.tile([P, HEAD], F32, tag="h_t")
+            nc.vector.scalar_tensor_tensor(
+                out=h_t[:], in0=o_gate[:], scalar=inv_denom[:, 0:1], in1=cq_all[:, cols],
+                op0=ALU.mult, op1=ALU.mult,
+            )
+            nc.sync.dma_start(out=h_out[:, cols], in_=h_t[:])

@@ -23,7 +23,7 @@ PASSES = D // K_PASS
 QUADS = 4
 LIVE = 4
 
-BQ, BK, BV, BI, BF, BO = range(6)
+BIAS_ORDER = ("q", "k", "v", "i", "o", "f")
 
 FLOPS = 2 * P * (3 * D * D + 3 * HEADS * HEAD * HEAD)
 
@@ -39,36 +39,48 @@ def tile_mlstmblock_pb_kernel(
 ):
     nc = tc.nc
     h_out, c_out, n_out, m_out = out_0, out_1, out_2, out_3
+    head_weight = {"q": wq_w, "k": wk_w, "v": wv_w}
+    packed_words = {"i": wi_w_words, "f": wf_w_words, "o": wo_w_words}
+    bias_vector = {"q": wq_b, "k": wk_b, "v": wv_b, "i": wi_b, "f": wf_b, "o": wo_b}
 
     with ExitStack() as ctx:
         const = ctx.enter_context(tc.tile_pool(name="const", bufs=1))
-        raw_pool = ctx.enter_context(tc.tile_pool(name="raw", bufs=6))
+        raw_pool = ctx.enter_context(tc.tile_pool(name="raw", bufs=8))
         grouped_pool = ctx.enter_context(tc.tile_pool(name="grouped", bufs=3))
         head_w_pool = ctx.enter_context(tc.tile_pool(name="head_w", bufs=4))
         packed_pool = ctx.enter_context(tc.tile_pool(name="packed", bufs=8))
         work = ctx.enter_context(tc.tile_pool(name="work", bufs=2))
         stored = ctx.enter_context(tc.tile_pool(name="stored", bufs=3))
-        acc_pool = ctx.enter_context(tc.psum_pool(name="acc", bufs=6))
-        aux_pool = ctx.enter_context(tc.psum_pool(name="aux", bufs=2))
+        psum = ctx.enter_context(tc.psum_pool(name="psum", bufs=8))
+        ctx.enter_context(tc.manual_schedule())
+
+        def columns(h):
+            return slice(HEAD * h, HEAD * (h + 1))
+
+        raw_of = {}
+        packed_of = {}
 
         def load_rows(src):
             rows = raw_pool.tile([P, D], BF16, tag="raw")
             nc.sync.dma_start(out=rows[:], in_=src)
             return rows
 
-        def load_head_weight(w, h):
-            raw = raw_pool.tile([P, PACK, HEAD], BF16, tag="raw")
-            nc.sync.dma_start(out=raw[:], in_=w[h].rearrange("(p t) o -> p t o", t=PACK))
-            return raw
+        def load_head_weights(h):
+            for name in ("k", "v", "q"):
+                raw = raw_pool.tile([P, PACK, HEAD], BF16, tag="raw")
+                nc.sync.dma_start(
+                    out=raw[:], in_=head_weight[name][h].rearrange("(p t) o -> p t o", t=PACK)
+                )
+                raw_of[h, name] = raw
 
-        def load_packed_columns(words, h):
+        def load_packed_columns(h, name):
             packed = packed_pool.tile([P, PASSES, HEAD], I32, tag="packed", align_bytes=64)
-            by_partition = words.rearrange("g p n t -> p g (n t)")
+            by_partition = packed_words[name].rearrange("g p n t -> p g (n t)")
             nc.sync.dma_start(
                 out=packed[:],
                 in_=by_partition[:, :, PACK * HEAD * h : PACK * HEAD * (h + 1)].bitcast(I32),
             )
-            return packed
+            packed_of[h, name] = packed
 
         def load_scale_planes(scales, planes):
             for quad in range(QUADS):
@@ -77,19 +89,23 @@ def tile_mlstmblock_pb_kernel(
                     in_=scales[:, LIVE * quad : LIVE * (quad + 1), :].bitcast(I32),
                 )
 
-        ident_f32 = const.tile([P, P], F32)
-        make_identity(nc, ident_f32[:])
         ident_bf16 = const.tile([P, P], BF16)
         make_identity(nc, ident_bf16[:])
+        ident_f32 = const.tile([P, P], F32)
+        make_identity(nc, ident_f32[:])
         half = const.tile([P, 1], F32)
         nc.vector.memset(half[:], 0.5)
 
+        warm = const.tile([P, 1], F32)
+        nc.vector.memset(warm[:], 0.0)
+        nc.scalar.activation(out=warm[:], in_=warm[:], func=ACT.Exp)
+
         bias_rows = const.tile([P, HEAD], BF16)
         nc.vector.memset(bias_rows[:], 0.0)
-        for j, bias in enumerate((wq_b, wk_b, wv_b, wi_b, wf_b, wo_b)):
+        for j, name in enumerate(BIAS_ORDER):
             nc.sync.dma_start(
                 out=bias_rows[HEADS * j : HEADS * (j + 1), :],
-                in_=bias.rearrange("(h c) -> h c", c=HEAD),
+                in_=bias_vector[name].rearrange("(h c) -> h c", c=HEAD),
             )
 
         planes_i = const.tile([P, D], U8, align_bytes=64)
@@ -100,30 +116,47 @@ def tile_mlstmblock_pb_kernel(
 
         xc_rows = load_rows(x_conv)
         xl_rows = load_rows(x_left)
-        m_rows = load_rows(m_prev)
-        head_raw = {}
-        gate_packed = {}
-
-        def load_head(h):
-            head_raw[h] = (
-                load_head_weight(wk_w, h),
-                load_head_weight(wv_w, h),
-                load_head_weight(wq_w, h),
-            )
-            if h == 0:
-                load_scale_planes(wi_w_scales, planes_i)
-                load_scale_planes(wf_w_scales, planes_f)
-                load_scale_planes(wo_w_scales, planes_o)
-            gate_packed[h] = (
-                load_packed_columns(wi_w_words, h),
-                load_packed_columns(wf_w_words, h),
-            )
-
-        load_head(0)
+        load_head_weights(0)
+        load_head_weights(1)
+        m_rows = const.tile([P, D], BF16)
+        nc.sync.dma_start(out=m_rows[:], in_=m_prev)
+        load_scale_planes(wi_w_scales, planes_i)
+        load_scale_planes(wf_w_scales, planes_f)
+        load_packed_columns(0, "i")
+        load_packed_columns(0, "f")
         c_rows = const.tile([P, D], BF16)
         nc.sync.dma_start(out=c_rows[:], in_=c_prev)
         n_rows = const.tile([P, D], BF16)
         nc.sync.dma_start(out=n_rows[:], in_=n_prev)
+        load_scale_planes(wo_w_scales, planes_o)
+
+        bias_all = const.tile([P, HEADS, 5, HEAD], BF16)
+        fbias_m = const.tile([P, D], F32)
+        fbias_spread = {}
+
+        def spread_biases(h):
+            for pair in range(3):
+                spread = psum.tile([P, 2, HEAD], BF16, tag="bank")
+                for i in range(2):
+                    row = HEADS * (2 * pair + i) + h
+                    nc.tensor.matmul(
+                        out=spread[:, i, :],
+                        lhsT=ident_bf16[:, row : row + 1].to_broadcast([P, P]),
+                        rhs=bias_rows[:],
+                        start=True,
+                        stop=True,
+                    )
+                if pair < 2:
+                    nc.scalar.copy(out=bias_all[:, h, 2 * pair : 2 * pair + 2, :], in_=spread[:])
+                else:
+                    nc.scalar.copy(out=bias_all[:, h, 4, :], in_=spread[:, 0, :])
+                    fbias_spread[h] = spread
+
+        def add_m_prev(h):
+            nc.vector.tensor_tensor(
+                out=fbias_m[:, columns(h)], in0=fbias_spread[h][:, 1, :],
+                in1=m_rows[:, columns(h)], op=ALU.add,
+            )
 
         def quantise_rows(rows, codes, plane):
             words = rows[:].bitcast(F32)
@@ -132,7 +165,7 @@ def tile_mlstmblock_pb_kernel(
                 "p (g b u) -> p g b u", g=PASSES, u=2
             )
             for pair in range(PASSES // 2):
-                turned = aux_pool.tile([P, 2, 2, P], F32, tag="aux")
+                turned = psum.tile([P, 2, 2, P], F32, tag="bank")
                 for i in range(2):
                     g = 2 * pair + i
                     for u in range(2):
@@ -150,44 +183,37 @@ def tile_mlstmblock_pb_kernel(
 
         xc_codes = const.tile([P, PASSES * P], U32, align_bytes=64)
         xc_plane = const.tile([P, PASSES * P], U8, align_bytes=64)
-        quantise_rows(xc_rows, xc_codes, xc_plane)
         xl_codes = const.tile([P, PASSES * P], U32, align_bytes=64)
         xl_plane = const.tile([P, PASSES * P], U8, align_bytes=64)
-        quantise_rows(xl_rows, xl_codes, xl_plane)
 
-        bias_all = const.tile([P, HEADS, 6, HEAD], BF16)
-        for h in range(HEADS):
-            for pair in range(3):
-                spread = aux_pool.tile([P, 2, HEAD], BF16, tag="aux")
-                for i in range(2):
-                    row = HEADS * (2 * pair + i) + h
-                    nc.tensor.matmul(
-                        out=spread[:, i, :],
-                        lhsT=ident_bf16[:, row : row + 1].to_broadcast([P, P]),
-                        rhs=bias_rows[:],
-                        start=True,
-                        stop=True,
-                    )
-                copy = nc.scalar.copy if (3 * h + pair) % 2 == 0 else nc.vector.tensor_copy
-                copy(out=bias_all[:, h, 2 * pair : 2 * pair + 2, :], in_=spread[:])
+        x_conv_mx, x_left_mx = (xc_codes, xc_plane), (xl_codes, xl_plane)
+        x_of = {"k": x_conv_mx, "q": x_conv_mx, "i": x_conv_mx, "f": x_conv_mx,
+                "v": x_left_mx, "o": x_left_mx}
+        planes_of = {"i": planes_i, "f": planes_f, "o": planes_o}
+        grouped_of = {}
+        quantised = {}
+        acc_of = {}
 
-        fbias_m = const.tile([P, D], F32)
-        for h in range(HEADS):
-            cols = slice(HEAD * h, HEAD * (h + 1))
-            nc.vector.tensor_tensor(
-                out=fbias_m[:, cols], in0=m_rows[:, cols], in1=bias_all[:, h, BF, :], op=ALU.add
-            )
-
-        def project_head(raw, x_codes, x_plane, h):
+        def regroup(h, name, copy):
             grouped = grouped_pool.tile([P, PACK * HEAD], BF16, tag="grouped", align_bytes=64)
-            nc.scalar.copy(
+            copy(
                 out=grouped[:].rearrange("p (c i t) -> p c t i", i=4, t=PACK),
-                in_=raw[:].rearrange("p t (c i) -> p c t i", i=4),
+                in_=raw_of[h, name][:].rearrange("p t (c i) -> p c t i", i=4),
             )
+            grouped_of[h, name] = grouped
+
+        def quantise(h, name):
             codes = head_w_pool.tile([P, HEAD], U32, tag="codes", align_bytes=64)
             plane = head_w_pool.tile([P, HEAD], U8, tag="plane", align_bytes=64)
-            nc.vector.quantize_mx(out=codes[:].bitcast(FP8X4), scales=plane[:], in_=grouped[:])
-            acc = acc_pool.tile([P, HEAD], F32, tag="acc")
+            nc.vector.quantize_mx(
+                out=codes[:].bitcast(FP8X4), scales=plane[:], in_=grouped_of[h, name][:]
+            )
+            quantised[h, name] = (codes, plane)
+
+        def project_head(h, name):
+            x_codes, x_plane = x_of[name]
+            codes, plane = quantised[h, name]
+            acc = psum.tile([P, HEAD], F32, tag="bank")
             rows = slice(P * h, P * (h + 1))
             nc.tensor.matmul_mx(
                 out=acc[:],
@@ -198,110 +224,180 @@ def tile_mlstmblock_pb_kernel(
                 start=True,
                 stop=True,
             )
-            return acc
+            acc_of[h, name] = acc
 
-        def project_full(packed, planes, x_codes, x_plane, h):
-            acc = acc_pool.tile([P, HEAD], F32, tag="acc")
+        def project_full(h, name):
+            x_codes, x_plane = x_of[name]
+            acc = psum.tile([P, HEAD], F32, tag="bank")
             for g in range(PASSES):
                 rows = slice(P * g, P * (g + 1))
                 nc.tensor.matmul_mx(
                     out=acc[:],
                     lhsT=x_codes[:, rows].bitcast(FP8X4),
                     lhsT_scale=x_plane[:, rows],
-                    rhs=packed[:, g, :].bitcast(FP8X4),
-                    rhs_scale=planes[LIVE * g : P, HEAD * h : HEAD * (h + 1)],
+                    rhs=packed_of[h, name][:, g, :].bitcast(FP8X4),
+                    rhs_scale=planes_of[name][LIVE * g : P, columns(h)],
                     start=(g == 0),
                     stop=(g == PASSES - 1),
                 )
-            return acc
+            acc_of[h, name] = acc
 
-        def add_bias(acc, h, which, tag):
-            biased = work.tile([P, HEAD], F32, tag=tag)
+        def add_bias(h, name, bufs):
+            biased = work.tile([P, HEAD], F32, tag=name, bufs=bufs)
             nc.vector.tensor_tensor(
-                out=biased[:], in0=acc[:], in1=bias_all[:, h, which, :], op=ALU.add
+                out=biased[:], in0=acc_of[h, name][:],
+                in1=bias_all[:, h, BIAS_ORDER.index(name), :], op=ALU.add,
             )
             return biased
 
         cq_all = const.tile([P, D], F32)
         square_sums = const.tile([P, HEADS], F32)
+        gate = {}
+        biased_of = {}
+        nq_of = {}
+        new_state = {}
 
-        def update_head(h):
-            cols = slice(HEAD * h, HEAD * (h + 1))
-            k_raw, v_raw, q_raw = head_raw[h]
-            i_packed, f_packed = gate_packed[h]
-            k_acc = project_head(k_raw, xc_codes, xc_plane, h)
-            v_acc = project_head(v_raw, xl_codes, xl_plane, h)
-            q_acc = project_head(q_raw, xc_codes, xc_plane, h)
-            i_acc = project_full(i_packed, planes_i, xc_codes, xc_plane, h)
-            f_acc = project_full(f_packed, planes_f, xc_codes, xc_plane, h)
-
-            k = add_bias(k_acc, h, BK, "k")
-            v = add_bias(v_acc, h, BV, "v")
-            q = add_bias(q_acc, h, BQ, "q")
-            i_gate = add_bias(i_acc, h, BI, "i_gate")
-            f_gate = work.tile([P, HEAD], F32, tag="f_gate")
+        def gate_arguments(h):
+            i_gate = add_bias(h, "i", 2)
+            f_gate = work.tile([P, HEAD], F32, tag="f")
             nc.vector.tensor_tensor(
-                out=f_gate[:], in0=f_acc[:], in1=fbias_m[:, cols], op=ALU.add
+                out=f_gate[:], in0=acc_of[h, "f"][:], in1=fbias_m[:, columns(h)], op=ALU.add
             )
-
             m_t = stored.tile([P, HEAD], F32, tag="m_t")
             nc.vector.tensor_tensor(out=m_t[:], in0=f_gate[:], in1=i_gate[:], op=ALU.max)
-            nc.sync.dma_start(out=m_out[:, cols], in_=m_t[:])
+            nc.vector.tensor_tensor(out=i_gate[:], in0=i_gate[:], in1=f_gate[:], op=ALU.subtract)
+            new_state[h, "m"] = m_t
+            gate[h, "i"] = i_gate
+            gate[h, "f"] = f_gate
 
-            nc.vector.tensor_tensor(out=i_gate[:], in0=i_gate[:], in1=m_t[:], op=ALU.subtract)
-            nc.vector.tensor_tensor(out=f_gate[:], in0=f_gate[:], in1=m_t[:], op=ALU.subtract)
-            nc.scalar.activation(out=i_gate[:], in_=i_gate[:], func=ACT.Exp)
-            nc.scalar.activation(out=f_gate[:], in_=f_gate[:], func=ACT.Exp)
+        def gate_exponentials(h):
+            d = gate[h, "i"]
+            nc.scalar.activation(out=gate[h, "f"][:], in_=d[:], func=ACT.Exp, scale=-1.0)
+            nc.scalar.activation(out=d[:], in_=d[:], func=ACT.Exp)
 
+        def update_state(h):
+            cols = columns(h)
+            exp_i, exp_f = gate[h, "i"], gate[h, "f"]
+            k, v, q = biased_of[h, "k"], biased_of[h, "v"], biased_of[h, "q"]
+            k_scale = 1.0 / math.sqrt(HEAD)
+            c_t = stored.tile([P, HEAD], F32, tag="c_t")
+            n_t = stored.tile([P, HEAD], F32, tag="n_t")
             nc.vector.scalar_tensor_tensor(
-                out=k[:], in0=k[:], scalar=1.0 / math.sqrt(HEAD), in1=i_gate[:],
-                op0=ALU.mult, op1=ALU.mult,
+                out=n_t[:], in0=exp_f[:], scalar=1.0, in1=n_rows[:, cols],
+                op0=ALU.min, op1=ALU.mult,
+            )
+            nc.vector.scalar_tensor_tensor(
+                out=k[:], in0=exp_i[:], scalar=1.0, in1=k[:], op0=ALU.min, op1=ALU.mult
+            )
+            nc.vector.scalar_tensor_tensor(
+                out=c_t[:], in0=exp_f[:], scalar=1.0, in1=c_rows[:, cols],
+                op0=ALU.min, op1=ALU.mult,
             )
             nc.vector.tensor_tensor(out=v[:], in0=v[:], in1=k[:], op=ALU.mult)
-
-            c_t = stored.tile([P, HEAD], F32, tag="c_t")
-            nc.vector.tensor_tensor(out=c_t[:], in0=f_gate[:], in1=c_rows[:, cols], op=ALU.mult)
-            n_t = stored.tile([P, HEAD], F32, tag="n_t")
-            nc.vector.tensor_tensor(out=n_t[:], in0=f_gate[:], in1=n_rows[:, cols], op=ALU.mult)
-            nc.vector.tensor_tensor(out=c_t[:], in0=c_t[:], in1=v[:], op=ALU.add)
-            nc.vector.tensor_tensor(out=n_t[:], in0=n_t[:], in1=k[:], op=ALU.add)
-            nc.sync.dma_start(out=c_out[:, cols], in_=c_t[:])
-            nc.sync.dma_start(out=n_out[:, cols], in_=n_t[:])
-
+            nc.vector.scalar_tensor_tensor(
+                out=n_t[:], in0=k[:], scalar=k_scale, in1=n_t[:], op0=ALU.mult, op1=ALU.add
+            )
+            nc.vector.scalar_tensor_tensor(
+                out=c_t[:], in0=v[:], scalar=k_scale, in1=c_t[:], op0=ALU.mult, op1=ALU.add
+            )
             nq = work.tile([P, HEAD], F32, tag="nq")
             nc.vector.tensor_tensor(out=nq[:], in0=n_t[:], in1=q[:], op=ALU.mult)
+            nc.vector.tensor_tensor(out=cq_all[:, cols], in0=c_t[:], in1=q[:], op=ALU.mult)
+            nq_of[h] = nq
+            new_state[h, "c"] = c_t
+            new_state[h, "n"] = n_t
+
+        def sum_squares(h):
+            nq = nq_of[h]
             nc.scalar.activation(
                 out=nq[:], in_=nq[:], func=ACT.Square, accum_out=square_sums[:, h : h + 1]
             )
-            nc.vector.tensor_tensor(out=cq_all[:, cols], in0=c_t[:], in1=q[:], op=ALU.mult)
 
-        load_head(1)
-        update_head(0)
-        load_head(2)
-        update_head(1)
-        load_head(3)
-        o_packed = [load_packed_columns(wo_w_words, h) for h in range(HEADS)]
-        update_head(2)
-        update_head(3)
+        def store_state(h):
+            nc.sync.dma_start(out=m_out[:, columns(h)], in_=new_state[h, "m"][:])
+            nc.sync.dma_start(out=n_out[:, columns(h)], in_=new_state[h, "n"][:])
+            nc.sync.dma_start(out=c_out[:, columns(h)], in_=new_state[h, "c"][:])
+
+        def quantise_and_project(h):
+            for name in ("k", "v", "q"):
+                quantise(h, name)
+                project_head(h, name)
+
+        def bias_kvq(h):
+            for name in ("k", "v", "q"):
+                biased_of[h, name] = add_bias(h, name, 2)
+
+        spread_biases(0)
+        quantise_rows(xc_rows, xc_codes, xc_plane)
+        quantise_rows(xl_rows, xl_codes, xl_plane)
+        for name in ("k", "v", "q"):
+            regroup(0, name, nc.vector.tensor_copy)
+        spread_biases(1)
+        add_m_prev(0)
+        add_m_prev(1)
+        quantise_and_project(0)
+        for name in ("k", "v", "q"):
+            regroup(1, name, nc.scalar.copy)
+        load_head_weights(2)
+        load_packed_columns(1, "i")
+        load_packed_columns(1, "f")
+        bias_kvq(0)
+        project_full(0, "i")
+        project_full(0, "f")
+
+        o_gate = {}
+        for h in range(HEADS):
+            gate_arguments(h)
+            gate_exponentials(h)
+            if h + 2 < HEADS:
+                spread_biases(h + 2)
+            if h + 1 < HEADS:
+                quantise_and_project(h + 1)
+                project_full(h + 1, "i")
+                project_full(h + 1, "f")
+            else:
+                nc.scalar.activation(out=warm[:], in_=warm[:], func=ACT.Sigmoid)
+                for j in range(HEADS // 2):
+                    o_gate[j] = add_bias(j, "o", HEADS)
+                    nc.scalar.activation(out=o_gate[j][:], in_=o_gate[j][:], func=ACT.Sigmoid)
+            update_state(h)
+            if h + 2 < HEADS:
+                for name in ("k", "v", "q"):
+                    regroup(h + 2, name, nc.scalar.copy)
+            sum_squares(h)
+            if h + 2 < HEADS:
+                add_m_prev(h + 2)
+                load_packed_columns(h + 2, "i")
+                load_packed_columns(h + 2, "f")
+            if h + 3 < HEADS:
+                load_head_weights(h + 3)
+            if h + 2 == HEADS:
+                for j in range(HEADS):
+                    load_packed_columns(j, "o")
+            if h + 1 < HEADS:
+                bias_kvq(h + 1)
+            if h + 2 == HEADS:
+                for j in range(HEADS):
+                    project_full(j, "o")
+            store_state(h)
 
         total = const.tile([P, 1], F32)
-        nc.vector.tensor_reduce(
-            out=total[:], in_=square_sums[:], axis=mybir.AxisListType.X, op=ALU.add
-        )
         denom = const.tile([P, 1], F32)
-        nc.gpsimd.tensor_tensor(out=denom[:], in0=total[:], in1=half[:], op=ALU.pow)
+        for j in range(HEADS // 2, HEADS):
+            o_gate[j] = add_bias(j, "o", HEADS)
+            nc.scalar.activation(out=o_gate[j][:], in_=o_gate[j][:], func=ACT.Sigmoid)
+            if j == HEADS // 2:
+                nc.vector.tensor_reduce(
+                    out=total[:], in_=square_sums[:], axis=mybir.AxisListType.X, op=ALU.add
+                )
+                nc.gpsimd.tensor_tensor(out=denom[:], in0=total[:], in1=half[:], op=ALU.pow)
         nc.vector.tensor_scalar_add(out=denom[:], in0=denom[:], scalar1=1e-6)
         inv_denom = const.tile([P, 1], F32)
         nc.vector.reciprocal(out=inv_denom[:], in_=denom[:])
 
-        for h in range(HEADS):
-            cols = slice(HEAD * h, HEAD * (h + 1))
-            o_acc = project_full(o_packed[h], planes_o, xl_codes, xl_plane, h)
-            o_gate = add_bias(o_acc, h, BO, "o_gate")
-            nc.scalar.activation(out=o_gate[:], in_=o_gate[:], func=ACT.Sigmoid)
-            h_t = stored.tile([P, HEAD], F32, tag="h_t")
+        for j in range(HEADS):
             nc.vector.scalar_tensor_tensor(
-                out=h_t[:], in0=o_gate[:], scalar=inv_denom[:, 0:1], in1=cq_all[:, cols],
-                op0=ALU.mult, op1=ALU.mult,
+                out=o_gate[j][:], in0=o_gate[j][:], scalar=inv_denom[:, 0:1],
+                in1=cq_all[:, columns(j)], op0=ALU.mult, op1=ALU.mult,
             )
-            nc.sync.dma_start(out=h_out[:, cols], in_=h_t[:])
+            nc.sync.dma_start(out=h_out[:, columns(j)], in_=o_gate[j][:])

@@ -22,6 +22,7 @@ D = HEADS * HEAD
 PASSES = D // K_PASS
 QUADS = 4
 LIVE = 4
+AUX_BANKS = 3
 
 BIAS_ORDER = ("q", "k", "v", "i", "o", "f")
 
@@ -51,7 +52,7 @@ def tile_mlstmblock_pb_kernel(
         packed_pool = ctx.enter_context(tc.tile_pool(name="packed", bufs=8))
         work = ctx.enter_context(tc.tile_pool(name="work", bufs=2))
         stored = ctx.enter_context(tc.tile_pool(name="stored", bufs=3))
-        psum = ctx.enter_context(tc.psum_pool(name="psum", bufs=8))
+        psum = ctx.enter_context(tc.psum_pool(name="psum", bufs=1))
         ctx.enter_context(tc.manual_schedule())
 
         def columns(h):
@@ -65,8 +66,8 @@ def tile_mlstmblock_pb_kernel(
             nc.sync.dma_start(out=rows[:], in_=src)
             return rows
 
-        def load_head_weights(h):
-            for name in ("k", "v", "q"):
+        def load_head_weights(h, names):
+            for name in names:
                 raw = raw_pool.tile([P, PACK, HEAD], BF16, tag="raw")
                 nc.sync.dma_start(
                     out=raw[:], in_=head_weight[name][h].rearrange("(p t) o -> p t o", t=PACK)
@@ -116,47 +117,60 @@ def tile_mlstmblock_pb_kernel(
 
         xc_rows = load_rows(x_conv)
         xl_rows = load_rows(x_left)
-        load_head_weights(0)
-        load_head_weights(1)
+        load_head_weights(0, "kvq")
         m_rows = const.tile([P, D], BF16)
         nc.sync.dma_start(out=m_rows[:], in_=m_prev)
         load_scale_planes(wi_w_scales, planes_i)
         load_scale_planes(wf_w_scales, planes_f)
         load_packed_columns(0, "i")
         load_packed_columns(0, "f")
-        c_rows = const.tile([P, D], BF16)
-        nc.sync.dma_start(out=c_rows[:], in_=c_prev)
+        load_head_weights(1, "k")
         n_rows = const.tile([P, D], BF16)
         nc.sync.dma_start(out=n_rows[:], in_=n_prev)
-        load_scale_planes(wo_w_scales, planes_o)
+        c_rows = const.tile([P, D], BF16)
+        nc.sync.dma_start(out=c_rows[:], in_=c_prev)
+        load_head_weights(1, "vq")
+        load_packed_columns(1, "i")
+        load_packed_columns(1, "f")
 
-        bias_all = const.tile([P, HEADS, 5, HEAD], BF16)
-        fbias_m = const.tile([P, D], F32)
-        fbias_spread = {}
+        bias_qkvi = const.tile([P, HEADS, 4, HEAD], BF16)
+        bias_o = const.tile([P, HEADS, HEAD], BF16)
+        fbias_m = const.tile([P, HEADS, HEAD], F32)
 
-        def spread_biases(h):
-            for pair in range(3):
-                spread = psum.tile([P, 2, HEAD], BF16, tag="bank")
-                for i in range(2):
-                    row = HEADS * (2 * pair + i) + h
-                    nc.tensor.matmul(
-                        out=spread[:, i, :],
-                        lhsT=ident_bf16[:, row : row + 1].to_broadcast([P, P]),
-                        rhs=bias_rows[:],
-                        start=True,
-                        stop=True,
-                    )
-                if pair < 2:
-                    nc.scalar.copy(out=bias_all[:, h, 2 * pair : 2 * pair + 2, :], in_=spread[:])
-                else:
-                    nc.scalar.copy(out=bias_all[:, h, 4, :], in_=spread[:, 0, :])
-                    fbias_spread[h] = spread
+        def spread_two(rows):
+            spread = psum.tile([P, 2, HEAD], BF16, tag="aux", bufs=AUX_BANKS)
+            for i, r in enumerate(rows):
+                nc.tensor.matmul(
+                    out=spread[:, i, :],
+                    lhsT=ident_bf16[:, r : r + 1].to_broadcast([P, P]),
+                    rhs=bias_rows[:],
+                    start=True,
+                    stop=True,
+                )
+            return spread
 
-        def add_m_prev(h):
-            nc.vector.tensor_tensor(
-                out=fbias_m[:, columns(h)], in0=fbias_spread[h][:, 1, :],
-                in1=m_rows[:, columns(h)], op=ALU.add,
-            )
+        def bias_row(name, h):
+            return HEADS * BIAS_ORDER.index(name) + h
+
+        def spread_head_biases(h, copy):
+            for pair in (("q", "k"), ("v", "i")):
+                spread = spread_two([bias_row(name, h) for name in pair])
+                first = BIAS_ORDER.index(pair[0])
+                copy(out=bias_qkvi[:, h, first : first + 2, :], in_=spread[:])
+
+        def spread_o_biases(copy):
+            for h in range(0, HEADS, 2):
+                spread = spread_two([bias_row("o", h), bias_row("o", h + 1)])
+                copy(out=bias_o[:, h : h + 2, :], in_=spread[:])
+
+        def spread_f_biases():
+            for h in range(0, HEADS, 2):
+                spread = spread_two([bias_row("f", h), bias_row("f", h + 1)])
+                nc.vector.tensor_tensor(
+                    out=fbias_m[:, h : h + 2, :], in0=spread[:],
+                    in1=m_rows[:, HEAD * h : HEAD * (h + 2)].rearrange("p (h c) -> p h c", c=HEAD),
+                    op=ALU.add,
+                )
 
         def quantise_rows(rows, codes, plane):
             words = rows[:].bitcast(F32)
@@ -165,7 +179,7 @@ def tile_mlstmblock_pb_kernel(
                 "p (g b u) -> p g b u", g=PASSES, u=2
             )
             for pair in range(PASSES // 2):
-                turned = psum.tile([P, 2, 2, P], F32, tag="bank")
+                turned = psum.tile([P, 2, 2, P], F32, tag="aux", bufs=AUX_BANKS)
                 for i in range(2):
                     g = 2 * pair + i
                     for u in range(2):
@@ -174,8 +188,7 @@ def tile_mlstmblock_pb_kernel(
                             in_=words[:, 256 * g + u : 256 * (g + 1) : 2],
                             identity=ident_f32[:],
                         )
-                copy = nc.scalar.copy if pair == 0 else nc.vector.tensor_copy
-                copy(
+                nc.scalar.copy(
                     out=grouped_words[:, 2 * pair : 2 * pair + 2, :, :],
                     in_=turned[:].rearrange("p g u b -> p g b u"),
                 )
@@ -213,7 +226,7 @@ def tile_mlstmblock_pb_kernel(
         def project_head(h, name):
             x_codes, x_plane = x_of[name]
             codes, plane = quantised[h, name]
-            acc = psum.tile([P, HEAD], F32, tag="bank")
+            acc = psum.tile([P, HEAD], F32, tag=name)
             rows = slice(P * h, P * (h + 1))
             nc.tensor.matmul_mx(
                 out=acc[:],
@@ -228,7 +241,10 @@ def tile_mlstmblock_pb_kernel(
 
         def project_full(h, name):
             x_codes, x_plane = x_of[name]
-            acc = psum.tile([P, HEAD], F32, tag="bank")
+            if name == "o":
+                acc = psum.tile([P, HEAD], F32, tag="aux", bufs=AUX_BANKS)
+            else:
+                acc = psum.tile([P, HEAD], F32, tag=name)
             for g in range(PASSES):
                 rows = slice(P * g, P * (g + 1))
                 nc.tensor.matmul_mx(
@@ -244,10 +260,8 @@ def tile_mlstmblock_pb_kernel(
 
         def add_bias(h, name, bufs):
             biased = work.tile([P, HEAD], F32, tag=name, bufs=bufs)
-            nc.vector.tensor_tensor(
-                out=biased[:], in0=acc_of[h, name][:],
-                in1=bias_all[:, h, BIAS_ORDER.index(name), :], op=ALU.add,
-            )
+            bias = bias_o[:, h, :] if name == "o" else bias_qkvi[:, h, BIAS_ORDER.index(name), :]
+            nc.vector.tensor_tensor(out=biased[:], in0=acc_of[h, name][:], in1=bias, op=ALU.add)
             return biased
 
         cq_all = const.tile([P, D], F32)
@@ -261,7 +275,7 @@ def tile_mlstmblock_pb_kernel(
             i_gate = add_bias(h, "i", 2)
             f_gate = work.tile([P, HEAD], F32, tag="f")
             nc.vector.tensor_tensor(
-                out=f_gate[:], in0=acc_of[h, "f"][:], in1=fbias_m[:, columns(h)], op=ALU.add
+                out=f_gate[:], in0=acc_of[h, "f"][:], in1=fbias_m[:, h, :], op=ALU.add
             )
             m_t = stored.tile([P, HEAD], F32, tag="m_t")
             nc.vector.tensor_tensor(out=m_t[:], in0=f_gate[:], in1=i_gate[:], op=ALU.max)
@@ -327,59 +341,59 @@ def tile_mlstmblock_pb_kernel(
             for name in ("k", "v", "q"):
                 biased_of[h, name] = add_bias(h, name, 2)
 
-        spread_biases(0)
         quantise_rows(xc_rows, xc_codes, xc_plane)
         quantise_rows(xl_rows, xl_codes, xl_plane)
         for name in ("k", "v", "q"):
-            regroup(0, name, nc.vector.tensor_copy)
-        spread_biases(1)
-        add_m_prev(0)
-        add_m_prev(1)
+            regroup(0, name, nc.scalar.copy)
+        load_head_weights(2, "kvq")
+        load_packed_columns(2, "i")
+        load_packed_columns(2, "f")
+        spread_head_biases(0, nc.vector.tensor_copy)
+        spread_head_biases(1, nc.vector.tensor_copy)
+        spread_f_biases()
         quantise_and_project(0)
-        for name in ("k", "v", "q"):
-            regroup(1, name, nc.scalar.copy)
-        load_head_weights(2)
-        load_packed_columns(1, "i")
-        load_packed_columns(1, "f")
-        bias_kvq(0)
         project_full(0, "i")
         project_full(0, "f")
 
         o_gate = {}
         for h in range(HEADS):
+            if h + 1 < HEADS:
+                regroup(h + 1, "k", nc.scalar.copy)
             gate_arguments(h)
             gate_exponentials(h)
-            if h + 2 < HEADS:
-                spread_biases(h + 2)
+            bias_kvq(h)
             if h + 1 < HEADS:
-                quantise_and_project(h + 1)
-                project_full(h + 1, "i")
-                project_full(h + 1, "f")
-            else:
+                regroup(h + 1, "v", nc.scalar.copy)
+                regroup(h + 1, "q", nc.scalar.copy)
+            if h + 2 < HEADS:
+                spread_head_biases(h + 2, nc.scalar.copy)
+            if h + 1 == HEADS:
                 nc.scalar.activation(out=warm[:], in_=warm[:], func=ACT.Sigmoid)
                 for j in range(HEADS // 2):
                     o_gate[j] = add_bias(j, "o", HEADS)
                     nc.scalar.activation(out=o_gate[j][:], in_=o_gate[j][:], func=ACT.Sigmoid)
+                for j in range(AUX_BANKS, HEADS):
+                    project_full(j, "o")
             update_state(h)
-            if h + 2 < HEADS:
-                for name in ("k", "v", "q"):
-                    regroup(h + 2, name, nc.scalar.copy)
             sum_squares(h)
-            if h + 2 < HEADS:
-                add_m_prev(h + 2)
-                load_packed_columns(h + 2, "i")
-                load_packed_columns(h + 2, "f")
-            if h + 3 < HEADS:
-                load_head_weights(h + 3)
-            if h + 2 == HEADS:
+            if h == 0:
+                load_head_weights(3, "kvq")
+                load_packed_columns(3, "i")
+                load_packed_columns(3, "f")
+            store_state(h)
+            if h == 0:
+                load_scale_planes(wo_w_scales, planes_o)
+            if h + 1 < HEADS:
+                project_full(h + 1, "i")
+                project_full(h + 1, "f")
+                quantise_and_project(h + 1)
+            if h == 0:
                 for j in range(HEADS):
                     load_packed_columns(j, "o")
-            if h + 1 < HEADS:
-                bias_kvq(h + 1)
             if h + 2 == HEADS:
-                for j in range(HEADS):
+                spread_o_biases(nc.scalar.copy)
+                for j in range(AUX_BANKS):
                     project_full(j, "o")
-            store_state(h)
 
         total = const.tile([P, 1], F32)
         denom = const.tile([P, 1], F32)

@@ -103,11 +103,6 @@ def tile_mlstmblock_pb_kernel(
 
         bias_rows = const.tile([P, HEAD], BF16)
         nc.vector.memset(bias_rows[:], 0.0)
-        for j, name in enumerate(BIAS_ORDER):
-            nc.sync.dma_start(
-                out=bias_rows[HEADS * j : HEADS * (j + 1), :],
-                in_=bias_vector[name].rearrange("(h c) -> h c", c=HEAD),
-            )
 
         planes_i = const.tile([P, D], U8, align_bytes=64)
         planes_f = const.tile([P, D], U8, align_bytes=64)
@@ -117,6 +112,11 @@ def tile_mlstmblock_pb_kernel(
 
         xc_rows = load_rows(x_conv)
         xl_rows = load_rows(x_left)
+        for j, name in enumerate(BIAS_ORDER):
+            nc.sync.dma_start(
+                out=bias_rows[HEADS * j : HEADS * (j + 1), :],
+                in_=bias_vector[name].rearrange("(h c) -> h c", c=HEAD),
+            )
         load_head_weights(0, "kvq")
         m_rows = const.tile([P, D], BF16)
         nc.sync.dma_start(out=m_rows[:], in_=m_prev)
@@ -241,8 +241,10 @@ def tile_mlstmblock_pb_kernel(
 
         def project_full(h, name):
             x_codes, x_plane = x_of[name]
-            if name == "o":
+            if name == "o" and h < AUX_BANKS:
                 acc = psum.tile([P, HEAD], F32, tag="aux", bufs=AUX_BANKS)
+            elif name == "o":
+                acc = psum.tile([P, HEAD], F32, tag="k")
             else:
                 acc = psum.tile([P, HEAD], F32, tag=name)
             for g in range(PASSES):
@@ -369,9 +371,6 @@ def tile_mlstmblock_pb_kernel(
                 spread_head_biases(h + 2, nc.scalar.copy)
             if h + 1 == HEADS:
                 nc.scalar.activation(out=warm[:], in_=warm[:], func=ACT.Sigmoid)
-                for j in range(HEADS // 2):
-                    o_gate[j] = add_bias(j, "o", HEADS)
-                    nc.scalar.activation(out=o_gate[j][:], in_=o_gate[j][:], func=ACT.Sigmoid)
                 for j in range(AUX_BANKS, HEADS):
                     project_full(j, "o")
             update_state(h)
@@ -397,10 +396,10 @@ def tile_mlstmblock_pb_kernel(
 
         total = const.tile([P, 1], F32)
         denom = const.tile([P, 1], F32)
-        for j in range(HEADS // 2, HEADS):
+        for j in range(HEADS):
             o_gate[j] = add_bias(j, "o", HEADS)
             nc.scalar.activation(out=o_gate[j][:], in_=o_gate[j][:], func=ACT.Sigmoid)
-            if j == HEADS // 2:
+            if j == 0:
                 nc.vector.tensor_reduce(
                     out=total[:], in_=square_sums[:], axis=mybir.AxisListType.X, op=ALU.add
                 )

@@ -77,10 +77,13 @@ def tile_mlstmblock_pb_kernel(
         def load_packed_columns(h, name):
             packed = packed_pool.tile([P, PASSES, HEAD], I32, tag="packed", align_bytes=64)
             by_partition = packed_words[name].rearrange("g p n t -> p g (n t)")
-            nc.sync.dma_start(
-                out=packed[:],
-                in_=by_partition[:, :, PACK * HEAD * h : PACK * HEAD * (h + 1)].bitcast(I32),
-            )
+            for g in range(0, PASSES, 2):
+                nc.sync.dma_start(
+                    out=packed[:, g : g + 2, :],
+                    in_=by_partition[
+                        :, g : g + 2, PACK * HEAD * h : PACK * HEAD * (h + 1)
+                    ].bitcast(I32),
+                )
             packed_of[h, name] = packed
 
         def load_scale_planes(scales, planes):
@@ -270,7 +273,6 @@ def tile_mlstmblock_pb_kernel(
         square_sums = const.tile([P, HEADS], F32)
         gate = {}
         biased_of = {}
-        nq_of = {}
         new_state = {}
 
         def gate_arguments(h):
@@ -279,17 +281,18 @@ def tile_mlstmblock_pb_kernel(
             nc.vector.tensor_tensor(
                 out=f_gate[:], in0=acc_of[h, "f"][:], in1=fbias_m[:, h, :], op=ALU.add
             )
+            biased_of[h, "k"] = add_bias(h, "k", 2)
             m_t = stored.tile([P, HEAD], F32, tag="m_t")
             nc.vector.tensor_tensor(out=m_t[:], in0=f_gate[:], in1=i_gate[:], op=ALU.max)
-            nc.vector.tensor_tensor(out=i_gate[:], in0=i_gate[:], in1=f_gate[:], op=ALU.subtract)
+            d = work.tile([P, HEAD], F32, tag="d")
+            nc.vector.tensor_tensor(out=d[:], in0=i_gate[:], in1=f_gate[:], op=ALU.subtract)
             new_state[h, "m"] = m_t
-            gate[h, "i"] = i_gate
-            gate[h, "f"] = f_gate
+            gate[h, "d"], gate[h, "i"], gate[h, "f"] = d, i_gate, f_gate
 
         def gate_exponentials(h):
-            d = gate[h, "i"]
+            d = gate[h, "d"]
             nc.scalar.activation(out=gate[h, "f"][:], in_=d[:], func=ACT.Exp, scale=-1.0)
-            nc.scalar.activation(out=d[:], in_=d[:], func=ACT.Exp)
+            nc.scalar.activation(out=gate[h, "i"][:], in_=d[:], func=ACT.Exp)
 
         def update_state(h):
             cols = columns(h)
@@ -316,15 +319,14 @@ def tile_mlstmblock_pb_kernel(
             nc.vector.scalar_tensor_tensor(
                 out=c_t[:], in0=v[:], scalar=k_scale, in1=c_t[:], op0=ALU.mult, op1=ALU.add
             )
-            nq = work.tile([P, HEAD], F32, tag="nq")
+            nq = gate[h, "d"]
             nc.vector.tensor_tensor(out=nq[:], in0=n_t[:], in1=q[:], op=ALU.mult)
             nc.vector.tensor_tensor(out=cq_all[:, cols], in0=c_t[:], in1=q[:], op=ALU.mult)
-            nq_of[h] = nq
             new_state[h, "c"] = c_t
             new_state[h, "n"] = n_t
 
         def sum_squares(h):
-            nq = nq_of[h]
+            nq = gate[h, "d"]
             nc.scalar.activation(
                 out=nq[:], in_=nq[:], func=ACT.Square, accum_out=square_sums[:, h : h + 1]
             )
@@ -339,8 +341,8 @@ def tile_mlstmblock_pb_kernel(
                 quantise(h, name)
                 project_head(h, name)
 
-        def bias_kvq(h):
-            for name in ("k", "v", "q"):
+        def bias_vq(h):
+            for name in ("v", "q"):
                 biased_of[h, name] = add_bias(h, name, 2)
 
         quantise_rows(xc_rows, xc_codes, xc_plane)
@@ -363,7 +365,7 @@ def tile_mlstmblock_pb_kernel(
                 regroup(h + 1, "k", nc.scalar.copy)
             gate_arguments(h)
             gate_exponentials(h)
-            bias_kvq(h)
+            bias_vq(h)
             if h + 1 < HEADS:
                 regroup(h + 1, "v", nc.scalar.copy)
                 regroup(h + 1, "q", nc.scalar.copy)

@@ -24,7 +24,7 @@ QUADS = 4
 LIVE = 4
 AUX_BANKS = 3
 
-BIAS_ORDER = ("q", "k", "v", "i", "o", "f")
+BIAS_ORDER = ("q", "k", "v", "i", "f")
 
 FLOPS = 2 * P * (3 * D * D + 3 * HEADS * HEAD * HEAD)
 
@@ -106,6 +106,8 @@ def tile_mlstmblock_pb_kernel(
 
         bias_rows = const.tile([P, HEAD], BF16)
         nc.vector.memset(bias_rows[:], 0.0)
+        o_bias_rows = const.tile([P, HEAD], BF16)
+        nc.vector.memset(o_bias_rows[:], 0.0)
 
         planes_i = const.tile([P, D], U8, align_bytes=64)
         planes_f = const.tile([P, D], U8, align_bytes=64)
@@ -128,6 +130,9 @@ def tile_mlstmblock_pb_kernel(
         load_packed_columns(0, "i")
         load_packed_columns(0, "f")
         load_head_weights(1, "k")
+        nc.sync.dma_start(
+            out=o_bias_rows[0:HEADS, :], in_=wo_b.rearrange("(h c) -> h c", c=HEAD)
+        )
         n_rows = const.tile([P, D], BF16)
         nc.sync.dma_start(out=n_rows[:], in_=n_prev)
         c_rows = const.tile([P, D], BF16)
@@ -140,13 +145,13 @@ def tile_mlstmblock_pb_kernel(
         bias_o = const.tile([P, HEADS, HEAD], BF16)
         fbias_m = const.tile([P, HEADS, HEAD], F32)
 
-        def spread_two(rows):
+        def spread_two(rows, source):
             spread = psum.tile([P, 2, HEAD], BF16, tag="aux", bufs=AUX_BANKS)
             for i, r in enumerate(rows):
                 nc.tensor.matmul(
                     out=spread[:, i, :],
                     lhsT=ident_bf16[:, r : r + 1].to_broadcast([P, P]),
-                    rhs=bias_rows[:],
+                    rhs=source[:],
                     start=True,
                     stop=True,
                 )
@@ -155,25 +160,31 @@ def tile_mlstmblock_pb_kernel(
         def bias_row(name, h):
             return HEADS * BIAS_ORDER.index(name) + h
 
+        def spread_pair(h, pair):
+            return spread_two([bias_row(name, h) for name in pair], bias_rows)
+
+        def keep_pair(h, pair, spread, copy):
+            first = BIAS_ORDER.index(pair[0])
+            copy(out=bias_qkvi[:, h, first : first + 2, :], in_=spread[:])
+
         def spread_head_biases(h, copy):
             for pair in (("q", "k"), ("v", "i")):
-                spread = spread_two([bias_row(name, h) for name in pair])
-                first = BIAS_ORDER.index(pair[0])
-                copy(out=bias_qkvi[:, h, first : first + 2, :], in_=spread[:])
+                keep_pair(h, pair, spread_pair(h, pair), copy)
 
         def spread_o_biases(copy):
             for h in range(0, HEADS, 2):
-                spread = spread_two([bias_row("o", h), bias_row("o", h + 1)])
+                spread = spread_two([h, h + 1], o_bias_rows)
                 copy(out=bias_o[:, h : h + 2, :], in_=spread[:])
 
-        def spread_f_biases():
-            for h in range(0, HEADS, 2):
-                spread = spread_two([bias_row("f", h), bias_row("f", h + 1)])
-                nc.vector.tensor_tensor(
-                    out=fbias_m[:, h : h + 2, :], in0=spread[:],
-                    in1=m_rows[:, HEAD * h : HEAD * (h + 2)].rearrange("p (h c) -> p h c", c=HEAD),
-                    op=ALU.add,
-                )
+        def spread_f_bias(h):
+            return spread_two([bias_row("f", h), bias_row("f", h + 1)], bias_rows)
+
+        def add_m_prev(h, spread):
+            nc.vector.tensor_tensor(
+                out=fbias_m[:, h : h + 2, :], in0=spread[:],
+                in1=m_rows[:, HEAD * h : HEAD * (h + 2)].rearrange("p (h c) -> p h c", c=HEAD),
+                op=ALU.add,
+            )
 
         def quantise_rows(rows, codes, plane):
             words = rows[:].bitcast(F32)
@@ -191,7 +202,7 @@ def tile_mlstmblock_pb_kernel(
                             in_=words[:, 256 * g + u : 256 * (g + 1) : 2],
                             identity=ident_f32[:],
                         )
-                nc.scalar.copy(
+                nc.vector.tensor_copy(
                     out=grouped_words[:, 2 * pair : 2 * pair + 2, :, :],
                     in_=turned[:].rearrange("p g u b -> p g b u"),
                 )
@@ -352,12 +363,24 @@ def tile_mlstmblock_pb_kernel(
         load_head_weights(2, "kvq")
         load_packed_columns(2, "i")
         load_packed_columns(2, "f")
-        spread_head_biases(0, nc.vector.tensor_copy)
-        spread_head_biases(1, nc.vector.tensor_copy)
-        spread_f_biases()
-        quantise_and_project(0)
+        qk, vi = ("q", "k"), ("v", "i")
+        spread_qk = spread_pair(0, qk)
+        spread_vi = spread_pair(0, vi)
+        spread_f01 = spread_f_bias(0)
+        keep_pair(0, qk, spread_qk, nc.vector.tensor_copy)
+        spread_f23 = spread_f_bias(2)
+        keep_pair(0, vi, spread_vi, nc.vector.tensor_copy)
+        quantise(0, "k")
+        project_head(0, "k")
+        add_m_prev(0, spread_f01)
         project_full(0, "i")
+        quantise(0, "v")
+        project_head(0, "v")
+        add_m_prev(2, spread_f23)
+        spread_head_biases(1, nc.scalar.copy)
         project_full(0, "f")
+        quantise(0, "q")
+        project_head(0, "q")
 
         o_gate = {}
         for h in range(HEADS):

@@ -88,9 +88,9 @@ def tile_mlstmblock_pb_kernel(
 
         def load_scale_planes(scales, planes):
             for quad in range(QUADS):
-                nc.sync.dma_start(
-                    out=planes[32 * quad : 32 * quad + PASSES * LIVE, :].bitcast(I32),
-                    in_=scales[:, LIVE * quad : LIVE * (quad + 1), :].bitcast(I32),
+                nc.gpsimd.dma_start(
+                    out=planes[32 * quad : 32 * quad + PASSES * LIVE, :].bitcast(F32),
+                    in_=scales[:, LIVE * quad : LIVE * (quad + 1), :].bitcast(F32),
                 )
 
         ident_bf16 = const.tile([P, P], BF16)
@@ -117,6 +117,9 @@ def tile_mlstmblock_pb_kernel(
 
         xc_rows = load_rows(x_conv)
         xl_rows = load_rows(x_left)
+        load_scale_planes(wi_w_scales, planes_i)
+        load_scale_planes(wf_w_scales, planes_f)
+        load_scale_planes(wo_w_scales, planes_o)
         for j, name in enumerate(BIAS_ORDER):
             nc.sync.dma_start(
                 out=bias_rows[HEADS * j : HEADS * (j + 1), :],
@@ -125,8 +128,6 @@ def tile_mlstmblock_pb_kernel(
         load_head_weights(0, "kvq")
         m_rows = const.tile([P, D], BF16)
         nc.sync.dma_start(out=m_rows[:], in_=m_prev)
-        load_scale_planes(wi_w_scales, planes_i)
-        load_scale_planes(wf_w_scales, planes_f)
         load_packed_columns(0, "i")
         load_packed_columns(0, "f")
         load_head_weights(1, "k")
@@ -405,8 +406,6 @@ def tile_mlstmblock_pb_kernel(
                 load_packed_columns(3, "i")
                 load_packed_columns(3, "f")
             store_state(h)
-            if h == 0:
-                load_scale_planes(wo_w_scales, planes_o)
             if h + 1 < HEADS:
                 project_full(h + 1, "i")
                 project_full(h + 1, "f")

from contextlib import ExitStack
import math

import concourse.mybir as mybir
from concourse.masks import make_identity

F32 = mybir.dt.float32
BF16 = mybir.dt.bfloat16
I32 = mybir.dt.int32
U32 = mybir.dt.uint32
U8 = mybir.dt.uint8
FP8X4 = mybir.dt.float8_e4m3fn_x4
ALU = mybir.AluOpType
ACT = mybir.ActivationFunctionType

P = 128
PACK = 4
K_PASS = P * PACK
HEADS = 4
HEAD = 512
D = HEADS * HEAD
PASSES = D // K_PASS
QUADS = 4
LIVE = 4
AUX_BANKS = 3

BIAS_ORDER = ("q", "k", "v", "i", "f")

FLOPS = 2 * P * (3 * D * D + 3 * HEADS * HEAD * HEAD)


def tile_mlstmblock_pb_kernel(
    tc,
    x_conv, x_left, c_prev, n_prev, m_prev,
    wq_w, wq_b, wk_w, wk_b, wv_w, wv_b,
    wi_w_words, wi_w_scales, wi_b,
    wf_w_words, wf_w_scales, wf_b,
    wo_w_words, wo_w_scales, wo_b,
    out_0, out_1, out_2, out_3,
):
    nc = tc.nc
    h_out, c_out, n_out, m_out = out_0, out_1, out_2, out_3
    head_weight = {"q": wq_w, "k": wk_w, "v": wv_w}
    packed_words = {"i": wi_w_words, "f": wf_w_words, "o": wo_w_words}
    bias_vector = {"q": wq_b, "k": wk_b, "v": wv_b, "i": wi_b, "f": wf_b, "o": wo_b}

    with ExitStack() as ctx:
        const = ctx.enter_context(tc.tile_pool(name="const", bufs=1))
        raw_pool = ctx.enter_context(tc.tile_pool(name="raw", bufs=8))
        grouped_pool = ctx.enter_context(tc.tile_pool(name="grouped", bufs=3))
        head_w_pool = ctx.enter_context(tc.tile_pool(name="head_w", bufs=4))
        packed_pool = ctx.enter_context(tc.tile_pool(name="packed", bufs=8))
        work = ctx.enter_context(tc.tile_pool(name="work", bufs=2))
        stored = ctx.enter_context(tc.tile_pool(name="stored", bufs=3))
        psum = ctx.enter_context(tc.psum_pool(name="psum", bufs=1))
        ctx.enter_context(tc.manual_schedule())

        def columns(h):
            return slice(HEAD * h, HEAD * (h + 1))

        raw_of = {}
        packed_of = {}

        def load_rows(src):
            rows = raw_pool.tile([P, D], BF16, tag="raw")
            nc.sync.dma_start(out=rows[:], in_=src)
            return rows

        def load_head_weights(h, names):
            for name in names:
                raw = raw_pool.tile([P, PACK, HEAD], BF16, tag="raw")
                nc.sync.dma_start(
                    out=raw[:], in_=head_weight[name][h].rearrange("(p t) o -> p t o", t=PACK)
                )
                raw_of[h, name] = raw

        def load_packed_columns(h, name):
            packed = packed_pool.tile([P, PASSES, HEAD], I32, tag="packed", align_bytes=64)
            by_partition = packed_words[name].rearrange("g p n t -> p g (n t)")
            for g in range(0, PASSES, 2):
                nc.sync.dma_start(
                    out=packed[:, g : g + 2, :],
                    in_=by_partition[
                        :, g : g + 2, PACK * HEAD * h : PACK * HEAD * (h + 1)
                    ].bitcast(I32),
                )
            packed_of[h, name] = packed

        def load_scale_planes(scales, planes):
            for quad in range(QUADS):
                nc.gpsimd.dma_start(
                    out=planes[32 * quad : 32 * quad + PASSES * LIVE, :].bitcast(F32),
                    in_=scales[:, LIVE * quad : LIVE * (quad + 1), :].bitcast(F32),
                )

        ident_bf16 = const.tile([P, P], BF16)
        make_identity(nc, ident_bf16[:])
        ident_f32 = const.tile([P, P], F32)
        make_identity(nc, ident_f32[:])
        half = const.tile([P, 1], F32)
        nc.vector.memset(half[:], 0.5)

        warm = const.tile([P, 1], F32)
        nc.vector.memset(warm[:], 0.0)
        nc.scalar.activation(out=warm[:], in_=warm[:], func=ACT.Exp)

        bias_rows = const.tile([P, HEAD], BF16)
        nc.vector.memset(bias_rows[:], 0.0)
        o_bias_rows = const.tile([P, HEAD], BF16)
        nc.vector.memset(o_bias_rows[:], 0.0)

        planes_i = const.tile([P, D], U8, align_bytes=64)
        planes_f = const.tile([P, D], U8, align_bytes=64)
        planes_o = const.tile([P, D], U8, align_bytes=64)
        for planes in (planes_i, planes_f, planes_o):
            nc.vector.memset(planes[:].bitcast(I32), 0)

        xc_rows = load_rows(x_conv)
        xl_rows = load_rows(x_left)
        load_scale_planes(wi_w_scales, planes_i)
        load_scale_planes(wf_w_scales, planes_f)
        load_scale_planes(wo_w_scales, planes_o)
        for j, name in enumerate(BIAS_ORDER):
            nc.sync.dma_start(
                out=bias_rows[HEADS * j : HEADS * (j + 1), :],
                in_=bias_vector[name].rearrange("(h c) -> h c", c=HEAD),
            )
        load_head_weights(0, "kvq")
        m_rows = const.tile([P, D], BF16)
        nc.sync.dma_start(out=m_rows[:], in_=m_prev)
        load_packed_columns(0, "i")
        load_packed_columns(0, "f")
        load_head_weights(1, "k")
        nc.sync.dma_start(
            out=o_bias_rows[0:HEADS, :], in_=wo_b.rearrange("(h c) -> h c", c=HEAD)
        )
        n_rows = const.tile([P, D], BF16)
        nc.sync.dma_start(out=n_rows[:], in_=n_prev)
        c_rows = const.tile([P, D], BF16)
        nc.sync.dma_start(out=c_rows[:], in_=c_prev)
        load_head_weights(1, "vq")
        load_packed_columns(1, "i")
        load_packed_columns(1, "f")

        bias_qkvi = const.tile([P, HEADS, 4, HEAD], BF16)
        bias_o = const.tile([P, HEADS, HEAD], BF16)
        fbias_m = const.tile([P, HEADS, HEAD], F32)

        def spread_two(rows, source):
            spread = psum.tile([P, 2, HEAD], BF16, tag="aux", bufs=AUX_BANKS)
            for i, r in enumerate(rows):
                nc.tensor.matmul(
                    out=spread[:, i, :],
                    lhsT=ident_bf16[:, r : r + 1].to_broadcast([P, P]),
                    rhs=source[:],
                    start=True,
                    stop=True,
                )
            return spread

        def bias_row(name, h):
            return HEADS * BIAS_ORDER.index(name) + h

        def spread_pair(h, pair):
            return spread_two([bias_row(name, h) for name in pair], bias_rows)

        def keep_pair(h, pair, spread, copy):
            first = BIAS_ORDER.index(pair[0])
            copy(out=bias_qkvi[:, h, first : first + 2, :], in_=spread[:])

        def spread_head_biases(h, copy):
            for pair in (("q", "k"), ("v", "i")):
                keep_pair(h, pair, spread_pair(h, pair), copy)

        def spread_o_biases(copy):
            for h in range(0, HEADS, 2):
                spread = spread_two([h, h + 1], o_bias_rows)
                copy(out=bias_o[:, h : h + 2, :], in_=spread[:])

        def spread_f_bias(h):
            return spread_two([bias_row("f", h), bias_row("f", h + 1)], bias_rows)

        def add_m_prev(h, spread):
            nc.vector.tensor_tensor(
                out=fbias_m[:, h : h + 2, :], in0=spread[:],
                in1=m_rows[:, HEAD * h : HEAD * (h + 2)].rearrange("p (h c) -> p h c", c=HEAD),
                op=ALU.add,
            )

        def quantise_rows(rows, codes, plane):
            words = rows[:].bitcast(F32)
            grouped = grouped_pool.tile([P, D], BF16, tag="grouped", align_bytes=64)
            grouped_words = grouped[:].bitcast(F32).rearrange(
                "p (g b u) -> p g b u", g=PASSES, u=2
            )
            for pair in range(PASSES // 2):
                turned = psum.tile([P, 2, 2, P], F32, tag="aux", bufs=AUX_BANKS)
                for i in range(2):
                    g = 2 * pair + i
                    for u in range(2):
                        nc.tensor.transpose(
                            out=turned[:, i, u, :],
                            in_=words[:, 256 * g + u : 256 * (g + 1) : 2],
                            identity=ident_f32[:],
                        )
                nc.vector.tensor_copy(
                    out=grouped_words[:, 2 * pair : 2 * pair + 2, :, :],
                    in_=turned[:].rearrange("p g u b -> p g b u"),
                )
            nc.vector.quantize_mx(out=codes[:].bitcast(FP8X4), scales=plane[:], in_=grouped[:])

        xc_codes = const.tile([P, PASSES * P], U32, align_bytes=64)
        xc_plane = const.tile([P, PASSES * P], U8, align_bytes=64)
        xl_codes = const.tile([P, PASSES * P], U32, align_bytes=64)
        xl_plane = const.tile([P, PASSES * P], U8, align_bytes=64)

        x_conv_mx, x_left_mx = (xc_codes, xc_plane), (xl_codes, xl_plane)
        x_of = {"k": x_conv_mx, "q": x_conv_mx, "i": x_conv_mx, "f": x_conv_mx,
                "v": x_left_mx, "o": x_left_mx}
        planes_of = {"i": planes_i, "f": planes_f, "o": planes_o}
        grouped_of = {}
        quantised = {}
        acc_of = {}

        def regroup(h, name, copy):
            grouped = grouped_pool.tile([P, PACK * HEAD], BF16, tag="grouped", align_bytes=64)
            copy(
                out=grouped[:].rearrange("p (c i t) -> p c t i", i=4, t=PACK),
                in_=raw_of[h, name][:].rearrange("p t (c i) -> p c t i", i=4),
            )
            grouped_of[h, name] = grouped

        def quantise(h, name):
            codes = head_w_pool.tile([P, HEAD], U32, tag="codes", align_bytes=64)
            plane = head_w_pool.tile([P, HEAD], U8, tag="plane", align_bytes=64)
            nc.vector.quantize_mx(
                out=codes[:].bitcast(FP8X4), scales=plane[:], in_=grouped_of[h, name][:]
            )
            quantised[h, name] = (codes, plane)

        def project_head(h, name):
            x_codes, x_plane = x_of[name]
            codes, plane = quantised[h, name]
            acc = psum.tile([P, HEAD], F32, tag=name)
            rows = slice(P * h, P * (h + 1))
            nc.tensor.matmul_mx(
                out=acc[:],
                lhsT=x_codes[:, rows].bitcast(FP8X4),
                lhsT_scale=x_plane[:, rows],
                rhs=codes[:].bitcast(FP8X4),
                rhs_scale=plane[:],
                start=True,
                stop=True,
            )
            acc_of[h, name] = acc

        def project_full(h, name):
            x_codes, x_plane = x_of[name]
            if name == "o" and h < AUX_BANKS:
                acc = psum.tile([P, HEAD], F32, tag="aux", bufs=AUX_BANKS)
            elif name == "o":
                acc = psum.tile([P, HEAD], F32, tag="k")
            else:
                acc = psum.tile([P, HEAD], F32, tag=name)
            for g in range(PASSES):
                rows = slice(P * g, P * (g + 1))
                nc.tensor.matmul_mx(
                    out=acc[:],
                    lhsT=x_codes[:, rows].bitcast(FP8X4),
                    lhsT_scale=x_plane[:, rows],
                    rhs=packed_of[h, name][:, g, :].bitcast(FP8X4),
                    rhs_scale=planes_of[name][LIVE * g : P, columns(h)],
                    start=(g == 0),
                    stop=(g == PASSES - 1),
                )
            acc_of[h, name] = acc

        def add_bias(h, name, bufs):
            biased = work.tile([P, HEAD], F32, tag=name, bufs=bufs)
            bias = bias_o[:, h, :] if name == "o" else bias_qkvi[:, h, BIAS_ORDER.index(name), :]
            nc.vector.tensor_tensor(out=biased[:], in0=acc_of[h, name][:], in1=bias, op=ALU.add)
            return biased

        cq_all = const.tile([P, D], F32)
        square_sums = const.tile([P, HEADS], F32)
        gate = {}
        biased_of = {}
        new_state = {}

        def gate_arguments(h):
            i_gate = add_bias(h, "i", 2)
            f_gate = work.tile([P, HEAD], F32, tag="f")
            nc.vector.tensor_tensor(
                out=f_gate[:], in0=acc_of[h, "f"][:], in1=fbias_m[:, h, :], op=ALU.add
            )
            biased_of[h, "k"] = add_bias(h, "k", 2)
            m_t = stored.tile([P, HEAD], F32, tag="m_t")
            nc.vector.tensor_tensor(out=m_t[:], in0=f_gate[:], in1=i_gate[:], op=ALU.max)
            d = work.tile([P, HEAD], F32, tag="d")
            nc.vector.tensor_tensor(out=d[:], in0=i_gate[:], in1=f_gate[:], op=ALU.subtract)
            new_state[h, "m"] = m_t
            gate[h, "d"], gate[h, "i"], gate[h, "f"] = d, i_gate, f_gate

        def gate_exponentials(h):
            d = gate[h, "d"]
            nc.scalar.activation(out=gate[h, "f"][:], in_=d[:], func=ACT.Exp, scale=-1.0)
            nc.scalar.activation(out=gate[h, "i"][:], in_=d[:], func=ACT.Exp)

        def update_state(h):
            cols = columns(h)
            exp_i, exp_f = gate[h, "i"], gate[h, "f"]
            k, v, q = biased_of[h, "k"], biased_of[h, "v"], biased_of[h, "q"]
            k_scale = 1.0 / math.sqrt(HEAD)
            c_t = stored.tile([P, HEAD], F32, tag="c_t")
            n_t = stored.tile([P, HEAD], F32, tag="n_t")
            nc.vector.scalar_tensor_tensor(
                out=n_t[:], in0=exp_f[:], scalar=1.0, in1=n_rows[:, cols],
                op0=ALU.min, op1=ALU.mult,
            )
            nc.vector.scalar_tensor_tensor(
                out=k[:], in0=exp_i[:], scalar=1.0, in1=k[:], op0=ALU.min, op1=ALU.mult
            )
            nc.vector.scalar_tensor_tensor(
                out=c_t[:], in0=exp_f[:], scalar=1.0, in1=c_rows[:, cols],
                op0=ALU.min, op1=ALU.mult,
            )
            nc.vector.tensor_tensor(out=v[:], in0=v[:], in1=k[:], op=ALU.mult)
            nc.vector.scalar_tensor_tensor(
                out=n_t[:], in0=k[:], scalar=k_scale, in1=n_t[:], op0=ALU.mult, op1=ALU.add
            )
            nc.vector.scalar_tensor_tensor(
                out=c_t[:], in0=v[:], scalar=k_scale, in1=c_t[:], op0=ALU.mult, op1=ALU.add
            )
            nq = gate[h, "d"]
            nc.vector.tensor_tensor(out=nq[:], in0=n_t[:], in1=q[:], op=ALU.mult)
            nc.vector.tensor_tensor(out=cq_all[:, cols], in0=c_t[:], in1=q[:], op=ALU.mult)
            new_state[h, "c"] = c_t
            new_state[h, "n"] = n_t

        def sum_squares(h):
            nq = gate[h, "d"]
            nc.scalar.activation(
                out=nq[:], in_=nq[:], func=ACT.Square, accum_out=square_sums[:, h : h + 1]
            )

        def store_state(h):
            nc.sync.dma_start(out=m_out[:, columns(h)], in_=new_state[h, "m"][:])
            nc.sync.dma_start(out=n_out[:, columns(h)], in_=new_state[h, "n"][:])
            nc.sync.dma_start(out=c_out[:, columns(h)], in_=new_state[h, "c"][:])

        def quantise_and_project(h):
            for name in ("k", "v", "q"):
                quantise(h, name)
                project_head(h, name)

        def bias_vq(h):
            for name in ("v", "q"):
                biased_of[h, name] = add_bias(h, name, 2)

        quantise_rows(xc_rows, xc_codes, xc_plane)
        quantise_rows(xl_rows, xl_codes, xl_plane)
        for name in ("k", "v", "q"):
            regroup(0, name, nc.scalar.copy)
        load_head_weights(2, "kvq")
        load_packed_columns(2, "i")
        load_packed_columns(2, "f")
        qk, vi = ("q", "k"), ("v", "i")
        spread_qk = spread_pair(0, qk)
        spread_vi = spread_pair(0, vi)
        spread_f01 = spread_f_bias(0)
        keep_pair(0, qk, spread_qk, nc.vector.tensor_copy)
        spread_f23 = spread_f_bias(2)
        keep_pair(0, vi, spread_vi, nc.vector.tensor_copy)
        quantise(0, "k")
        project_head(0, "k")
        add_m_prev(0, spread_f01)
        project_full(0, "i")
        quantise(0, "v")
        project_head(0, "v")
        add_m_prev(2, spread_f23)
        spread_head_biases(1, nc.scalar.copy)
        project_full(0, "f")
        quantise(0, "q")
        project_head(0, "q")

        o_gate = {}
        for h in range(HEADS):
            if h + 1 < HEADS:
                regroup(h + 1, "k", nc.scalar.copy)
            gate_arguments(h)
            gate_exponentials(h)
            bias_vq(h)
            if h + 1 < HEADS:
                regroup(h + 1, "v", nc.scalar.copy)
                regroup(h + 1, "q", nc.scalar.copy)
            if h + 2 < HEADS:
                spread_head_biases(h + 2, nc.scalar.copy)
            if h + 1 == HEADS:
                nc.scalar.activation(out=warm[:], in_=warm[:], func=ACT.Sigmoid)
                for j in range(AUX_BANKS, HEADS):
                    project_full(j, "o")
            update_state(h)
            sum_squares(h)
            if h == 0:
                load_head_weights(3, "kvq")
                load_packed_columns(3, "i")
                load_packed_columns(3, "f")
            store_state(h)
            if h + 1 < HEADS:
                project_full(h + 1, "i")
                project_full(h + 1, "f")
                quantise_and_project(h + 1)
            if h == 0:
                for j in range(HEADS):
                    load_packed_columns(j, "o")
            if h + 2 == HEADS:
                spread_o_biases(nc.scalar.copy)
                for j in range(AUX_BANKS):
                    project_full(j, "o")

        total = const.tile([P, 1], F32)
        denom = const.tile([P, 1], F32)
        for j in range(HEADS):
            o_gate[j] = add_bias(j, "o", HEADS)
            nc.scalar.activation(out=o_gate[j][:], in_=o_gate[j][:], func=ACT.Sigmoid)
            if j == 0:
                nc.vector.tensor_reduce(
                    out=total[:], in_=square_sums[:], axis=mybir.AxisListType.X, op=ALU.add
                )
                nc.gpsimd.tensor_tensor(out=denom[:], in0=total[:], in1=half[:], op=ALU.pow)
        nc.vector.tensor_scalar_add(out=denom[:], in0=denom[:], scalar1=1e-6)
        inv_denom = const.tile([P, 1], F32)
        nc.vector.reciprocal(out=inv_denom[:], in_=denom[:])

        for j in range(HEADS):
            nc.vector.scalar_tensor_tensor(
                out=o_gate[j][:], in0=o_gate[j][:], scalar=inv_denom[:, 0:1],
                in1=cq_all[:, columns(j)], op0=ALU.mult, op1=ALU.mult,
            )
            nc.sync.dma_start(out=h_out[:, columns(j)], in_=o_gate[j][:])
